import numpy as np
import ml_dtypes


def mxq(x, axis, fmt="e4m3"):
    dtype, down = {"e4m3": (ml_dtypes.float8_e4m3fn, 7), "e5m2": (ml_dtypes.float8_e5m2, 14)}[fmt]
    v = np.moveaxis(np.asarray(x, np.float32).astype(ml_dtypes.bfloat16).astype(np.float64), axis, -1)
    blocks = v.reshape(v.shape[:-1] + (-1, 32))
    amax = np.abs(blocks).max(-1, keepdims=True)
    byte = np.maximum(np.where(amax > 0, np.frexp(amax)[1] - 1 + 127, 0) - down, 1)
    scale = np.exp2(byte - 127.0)
    codes = (blocks / scale).astype(np.float32).astype(dtype).astype(np.float64)
    return np.moveaxis((codes * scale).reshape(v.shape), -1, axis)


WIDE = False


def mx_kscale(k):
    if not WIDE:
        return np.ones(k)
    levels = np.array([10, -10, 5, -5, 0])
    a = np.random.permutation(np.resize(levels, k // 512 * 4)).reshape(k // 512, 4)
    idx = np.arange(k)
    return np.exp2(a[idx // 512, idx % 128 // 32])


BF16 = ml_dtypes.bfloat16


def bf(x):
    return np.asarray(x, np.float32).astype(BF16)


def f64(x):
    return np.asarray(x).astype(np.float64)


E2M1 = np.array([0.0, 0.5, 1.0, 1.5, 2.0, 3.0, 4.0, 6.0, -0.0, -0.5, -1.0, -1.5, -2.0, -3.0, -4.0, -6.0])


def pack_weight(w, fmt):
    k, n = w.shape
    w = f64(bf(w)).reshape(k // 32, 32, n)
    amax = np.abs(w).max(1)
    if fmt == "e4m3":
        byte = np.frexp(amax)[1] - 1 + 127 - 7
    else:
        mant, ex = np.frexp(amax / 6.0)
        byte = np.where(mant > 0.5, ex, ex - 1) + 127
    byte = np.clip(np.where(amax > 0, byte, 1), 1, 254)
    scaled = (w * np.exp2(127.0 - byte)[:, None, :]).reshape(k, n).astype(np.float32)
    by_word = np.ascontiguousarray(scaled.reshape(k // 512, 128, 4, n).transpose(0, 1, 3, 2))
    if fmt == "e4m3":
        words = by_word.astype(ml_dtypes.float8_e4m3fn).view(np.uint8)
    else:
        c = by_word.astype(ml_dtypes.float4_e2m1fn).view(np.uint8) & 0xF
        words = c[..., 0::2] | (c[..., 1::2] << 4)
    return np.ascontiguousarray(words), np.ascontiguousarray(byte.astype(np.uint8).reshape(k // 512, 16, n))


def unpack_weight(words, scales, fmt):
    g, p, n, _ = words.shape
    if fmt == "e4m3":
        vals = np.ascontiguousarray(words).view(ml_dtypes.float8_e4m3fn).astype(np.float64)
    else:
        nib = np.empty((g, p, n, 4), np.uint8)
        nib[..., 0::2] = words & 0xF
        nib[..., 1::2] = words >> 4
        vals = E2M1[nib]
    vals = vals * np.repeat(np.exp2(scales.astype(np.float64) - 127.0), 8, axis=1)[..., None]
    return vals.transpose(0, 1, 3, 2).reshape(g * 512, n)


B, T, D, F = 4, 1024, 1024, 128
BINS = np.array([-1.5, -1.0, -0.5, 0.0, 0.5, 1.0, 1.5])
NB = BINS.shape[0] + 1
INDEX = 0


def setup_inputs():
    s = mx_kscale(D)
    s = s / s[INDEX]
    x = bf(np.random.standard_normal((B, T, D)) * s)
    stack = np.random.standard_normal((NB, D, F)) * 0.5 / np.sqrt(D) / s[None, :, None]
    cat = stack.reshape(-1, F)
    words, scales = pack_weight(cat, "e4m3")
    return {"x": x, "W_words": words, "W_scales": scales}


def reference(x, W_words, W_scales):
    x = f64(x)
    y = x[..., INDEX]
    mem = np.sum(np.where(y[..., None] > BINS, 1.0, 0.0), axis=-1)
    xf = x.reshape(B * T, D)
    memf = mem.reshape(B * T)
    xq = mxq(xf, 1, "e4m3")
    Wq = unpack_weight(W_words, W_scales, "e4m3").reshape(NB, D, F)
    out = np.zeros((B * T, F))
    for k in range(NB):
        sel = np.where(memf == k, 1.0, 0.0)[:, None]
        out = out + sel * (xq @ Wq[k])
    return out.reshape(B, T, F)

@@ -1,0 +1,185 @@
+from contextlib import ExitStack
+
+import concourse.mybir as mybir
+from concourse.masks import make_identity
+
+F32 = mybir.dt.float32
+BF16 = mybir.dt.bfloat16
+I32 = mybir.dt.int32
+U32 = mybir.dt.uint32
+U8 = mybir.dt.uint8
+FP8X4 = mybir.dt.float8_e4m3fn_x4
+ALU = mybir.AluOpType
+COPY = mybir.ActivationFunctionType.Copy
+
+P = 128
+TOKENS = 4 * 1024
+D = 1024
+F = 128
+EXPERTS = 8
+BINS = (-1.5, -1.0, -0.5, 0.0, 0.5, 1.0, 1.5)
+PACK = 4
+K_PASS = P * PACK
+PASSES = D // K_PASS
+WORDS_PASS = K_PASS // 2
+BANK_EXPERTS = 512 // F
+J = 4
+CHUNKS = TOKENS // (P * J)
+
+FLOPS = 2 * TOKENS * D * F * EXPERTS
+
+
+def tile_dispatchbyvariable_pa_t_e_kernel(tc, x, W_words, W_scales, out):
+    nc = tc.nc
+    x_chunks = x.rearrange("b t k -> (b t) k").rearrange("(c p j) k -> c p j k", p=P, j=J)
+    out_chunks = out.rearrange("b t f -> (b t) f").rearrange("(c p j) f -> c p j f", p=P, j=J)
+    words_in = W_words.rearrange("a p n t -> a p (n t)").bitcast(I32)
+    words_in = words_in.rearrange("(e g) p n -> g p e n", g=PASSES)
+    scales_in = W_scales.bitcast(I32).rearrange("a (h r) n -> r h a n", r=4)
+
+    with ExitStack() as ctx:
+        ctx.enter_context(tc.manual_schedule())
+        keep = ctx.enter_context(tc.tile_pool(name="keep", bufs=1))
+        work = ctx.enter_context(tc.tile_pool(name="work", bufs=2))
+        sums = ctx.enter_context(tc.tile_pool(name="sums", bufs=3))
+        psum_t = ctx.enter_context(tc.psum_pool(name="psum_t", bufs=J))
+        psum_mm = ctx.enter_context(tc.psum_pool(name="psum_mm", bufs=2))
+
+        x_sb = keep.tile([P, CHUNKS, J, D], BF16)
+        w_words = keep.tile([P, PASSES, EXPERTS, F], U32, align_bytes=64)
+        w_scales = keep.tile([P, PASSES, EXPERTS, F], U8, align_bytes=64)
+        scales_as_given = keep.tile([P, EXPERTS, PASSES, F], U8, align_bytes=64)
+        ident = keep.tile([P, P], F32)
+        bins = keep.tile([P, len(BINS)], F32)
+        greater = keep.tile([P, CHUNKS * J, EXPERTS + 1], F32)
+        factor = keep.tile([P, CHUNKS * J, EXPERTS], F32)
+
+        nc.vector.memset(scales_as_given[:].bitcast(I32), 0)
+        nc.sync.dma_start(out=x_sb[:, 0], in_=x_chunks[0])
+        for r in range(4):
+            nc.sync.dma_start(
+                out=scales_as_given[r:P:32].rearrange("h e g n -> h (e g) n").bitcast(I32),
+                in_=scales_in[r],
+            )
+        nc.sync.dma_start(out=x_sb[:, 1], in_=x_chunks[1])
+        for g in range(PASSES):
+            nc.sync.dma_start(out=w_words[:, g].bitcast(I32), in_=words_in[g])
+        for c in range(2, CHUNKS):
+            nc.sync.dma_start(out=x_sb[:, c], in_=x_chunks[c])
+
+        make_identity(nc, ident[:])
+        for b, bound in enumerate(BINS):
+            nc.vector.memset(bins[:, b : b + 1], bound)
+        nc.vector.memset(greater[:, :, 0:1], 1.0)
+        nc.vector.memset(greater[:, :, EXPERTS : EXPERTS + 1], 0.0)
+        nc.vector.tensor_copy(
+            out=w_scales[:].bitcast(I32),
+            in_=scales_as_given[:].bitcast(I32).rearrange("p e g n -> p g e n"),
+        )
+
+        def factors(c):
+            tiles = slice(c * J, (c + 1) * J)
+            shape = [P, J, len(BINS)]
+            nc.vector.tensor_tensor(
+                out=greater[:, tiles, 1:EXPERTS],
+                in0=x_sb[:, c, :, 0:1].to_broadcast(shape),
+                in1=bins[:].unsqueeze(1).to_broadcast(shape),
+                op=ALU.is_gt,
+            )
+            nc.vector.tensor_sub(
+                out=factor[:, tiles, :],
+                in0=greater[:, tiles, 0:EXPERTS],
+                in1=greater[:, tiles, 1 : EXPERTS + 1],
+            )
+
+        def transpose(c, j):
+            words = x_sb[:, c, j, :].bitcast(F32)
+            planes = psum_t.tile([P, PASSES * 2, P], F32)
+            for g in range(PASSES):
+                for u in range(2):
+                    nc.tensor.transpose(
+                        planes[:, 2 * g + u, :],
+                        words[:, WORDS_PASS * g + u : WORDS_PASS * (g + 1) : 2],
+                        ident[:],
+                    )
+            return planes
+
+        def regroup(planes, grouped, j):
+            nc.scalar.copy(
+                out=grouped[:, j].bitcast(F32),
+                in_=planes[:].rearrange("p (g u) n -> p g n u", u=2),
+            )
+
+        def quantise(grouped, codes, scales, j):
+            nc.vector.quantize_mx(
+                out=codes[:, j].rearrange("p g n -> p (g n)").bitcast(FP8X4),
+                scales=scales[:, j].rearrange("p g n -> p (g n)"),
+                in_=grouped[:, j].rearrange("p g n t -> p (g n t)"),
+            )
+
+        def multiply(codes, scales, j, first):
+            products = psum_mm.tile([P, BANK_EXPERTS, F], F32, tag="products%d" % first)
+            experts = slice(first, first + BANK_EXPERTS)
+            for g in range(PASSES):
+                nc.tensor.matmul_mx(
+                    out=products[:].rearrange("p e f -> p (e f)"),
+                    lhsT=codes[:, j, g, :].bitcast(FP8X4),
+                    lhsT_scale=scales[:, j, g, :],
+                    rhs=w_words[:, g, experts, :].rearrange("p e n -> p (e n)").bitcast(FP8X4),
+                    rhs_scale=w_scales[:, g, experts, :].rearrange("p e n -> p (e n)"),
+                    start=(g == 0),
+                    stop=(g == PASSES - 1),
+                )
+            return products
+
+        def new_operands():
+            grouped = work.tile([P, J, PASSES, P, PACK], BF16, align_bytes=64)
+            codes = work.tile([P, J, PASSES, P], U32, align_bytes=64)
+            scales = work.tile([P, J, PASSES, P], U8, align_bytes=64)
+            return grouped, codes, scales
+
+        factors(0)
+        grouped, codes, scales = new_operands()
+        for j in range(J):
+            regroup(transpose(0, j), grouped, j)
+        for j in range(J):
+            quantise(grouped, codes, scales, j)
+
+        for c in range(CHUNKS):
+            more = c + 1 < CHUNKS
+            if more:
+                factors(c + 1)
+                next_planes = [transpose(c + 1, j) for j in range(J)]
+                next_grouped, next_codes, next_scales = new_operands()
+            sum_even = sums.tile([P, J, F], F32)
+            sum_odd = sums.tile([P, J, F], F32)
+            running = (sum_even, sum_odd)
+            for j in range(J):
+                if more:
+                    regroup(next_planes[j], next_grouped, j)
+                for first in range(0, EXPERTS, BANK_EXPERTS):
+                    products = multiply(codes, scales, j, first)
+                    for e in range(first, first + BANK_EXPERTS):
+                        if e < 2:
+                            start = 1 - e
+                            nc.scalar.activation(
+                                out=running[start][:, j, :],
+                                in_=products[:, start, :],
+                                func=COPY,
+                                scale=factor[:, c * J + j, start : start + 1],
+                            )
+                        else:
+                            nc.vector.scalar_tensor_tensor(
+                                out=running[e % 2][:, j, :],
+                                in0=products[:, e - first, :],
+                                scalar=factor[:, c * J + j, e : e + 1],
+                                in1=running[e % 2][:, j, :],
+                                op0=ALU.mult,
+                                op1=ALU.add,
+                            )
+                if more:
+                    quantise(next_grouped, next_codes, next_scales, j)
+            nc.vector.tensor_add(out=sum_even[:], in0=sum_even[:], in1=sum_odd[:])
+            nc.sync.dma_start(out=out_chunks[c], in_=sum_even[:])
+            if more:
+                grouped, codes, scales = next_grouped, next_codes, next_scales

@@ -23,7 +23,8 @@ K_PASS = P * PACK
 PASSES = D // K_PASS
 WORDS_PASS = K_PASS // 2
 BANK_EXPERTS = 512 // F
-J = 4
+J = 2
+PSUM_BANKS = 8
 CHUNKS = TOKENS // (P * J)
 
 FLOPS = 2 * TOKENS * D * F * EXPERTS
@@ -41,9 +42,9 @@ def tile_dispatchbyvariable_pa_t_e_kernel(tc, x, W_words, W_scales, out):
         ctx.enter_context(tc.manual_schedule())
         keep = ctx.enter_context(tc.tile_pool(name="keep", bufs=1))
         work = ctx.enter_context(tc.tile_pool(name="work", bufs=2))
-        sums = ctx.enter_context(tc.tile_pool(name="sums", bufs=3))
+        sums = ctx.enter_context(tc.tile_pool(name="sums", bufs=4))
         psum_t = ctx.enter_context(tc.psum_pool(name="psum_t", bufs=J))
-        psum_mm = ctx.enter_context(tc.psum_pool(name="psum_mm", bufs=2))
+        psum_mm = ctx.enter_context(tc.psum_pool(name="psum_mm", bufs=(PSUM_BANKS - J) // 2))
 
         x_sb = keep.tile([P, CHUNKS, J, D], BF16)
         w_words = keep.tile([P, PASSES, EXPERTS, F], U32, align_bytes=64)

@@ -23,9 +23,9 @@ K_PASS = P * PACK
 PASSES = D // K_PASS
 WORDS_PASS = K_PASS // 2
 BANK_EXPERTS = 512 // F
-J = 2
-PSUM_BANKS = 8
+J = 4
 CHUNKS = TOKENS // (P * J)
+SUMS = 3
 
 FLOPS = 2 * TOKENS * D * F * EXPERTS
 
@@ -42,9 +42,9 @@ def tile_dispatchbyvariable_pa_t_e_kernel(tc, x, W_words, W_scales, out):
         ctx.enter_context(tc.manual_schedule())
         keep = ctx.enter_context(tc.tile_pool(name="keep", bufs=1))
         work = ctx.enter_context(tc.tile_pool(name="work", bufs=2))
-        sums = ctx.enter_context(tc.tile_pool(name="sums", bufs=4))
+        sums = ctx.enter_context(tc.tile_pool(name="sums", bufs=3))
         psum_t = ctx.enter_context(tc.psum_pool(name="psum_t", bufs=J))
-        psum_mm = ctx.enter_context(tc.psum_pool(name="psum_mm", bufs=(PSUM_BANKS - J) // 2))
+        psum_mm = ctx.enter_context(tc.psum_pool(name="psum_mm", bufs=2))
 
         x_sb = keep.tile([P, CHUNKS, J, D], BF16)
         w_words = keep.tile([P, PASSES, EXPERTS, F], U32, align_bytes=64)
@@ -152,35 +152,34 @@ def tile_dispatchbyvariable_pa_t_e_kernel(tc, x, W_words, W_scales, out):
                 factors(c + 1)
                 next_planes = [transpose(c + 1, j) for j in range(J)]
                 next_grouped, next_codes, next_scales = new_operands()
-            sum_even = sums.tile([P, J, F], F32)
-            sum_odd = sums.tile([P, J, F], F32)
-            running = (sum_even, sum_odd)
+            running = sums.tile([P, SUMS, J, F], F32)
+            result = sums.tile([P, J, F], F32)
             for j in range(J):
                 if more:
                     regroup(next_planes[j], next_grouped, j)
-                for first in range(0, EXPERTS, BANK_EXPERTS):
-                    products = multiply(codes, scales, j, first)
-                    for e in range(first, first + BANK_EXPERTS):
-                        if e < 2:
-                            start = 1 - e
-                            nc.scalar.activation(
-                                out=running[start][:, j, :],
-                                in_=products[:, start, :],
-                                func=COPY,
-                                scale=factor[:, c * J + j, start : start + 1],
-                            )
-                        else:
-                            nc.vector.scalar_tensor_tensor(
-                                out=running[e % 2][:, j, :],
-                                in0=products[:, e - first, :],
-                                scalar=factor[:, c * J + j, e : e + 1],
-                                in1=running[e % 2][:, j, :],
-                                op0=ALU.mult,
-                                op1=ALU.add,
-                            )
+                products = [multiply(codes, scales, j, first) for first in range(0, EXPERTS, BANK_EXPERTS)]
+                for e in reversed(range(SUMS)):
+                    nc.scalar.activation(
+                        out=running[:, e, j, :],
+                        in_=products[0][:, e, :],
+                        func=COPY,
+                        scale=factor[:, c * J + j, e : e + 1],
+                    )
+                for e in range(SUMS, EXPERTS):
+                    nc.vector.scalar_tensor_tensor(
+                        out=running[:, e % SUMS, j, :],
+                        in0=products[e // BANK_EXPERTS][:, e % BANK_EXPERTS, :],
+                        scalar=factor[:, c * J + j, e : e + 1],
+                        in1=running[:, e % SUMS, j, :],
+                        op0=ALU.mult,
+                        op1=ALU.add,
+                    )
+                last = (EXPERTS - 1) % SUMS
+                others = [i for i in range(SUMS) if i != last]
+                nc.gpsimd.tensor_add(out=result[:, j, :], in0=running[:, others[0], j, :], in1=running[:, others[1], j, :])
+                nc.gpsimd.tensor_add(out=result[:, j, :], in0=result[:, j, :], in1=running[:, last, j, :])
                 if more:
                     quantise(next_grouped, next_codes, next_scales, j)
-            nc.vector.tensor_add(out=sum_even[:], in0=sum_even[:], in1=sum_odd[:])
-            nc.sync.dma_start(out=out_chunks[c], in_=sum_even[:])
+            nc.sync.dma_start(out=out_chunks[c], in_=result[:])
             if more:
                 grouped, codes, scales = next_grouped, next_codes, next_scales

@@ -150,13 +150,12 @@ def tile_dispatchbyvariable_pa_t_e_kernel(tc, x, W_words, W_scales, out):
             more = c + 1 < CHUNKS
             if more:
                 factors(c + 1)
-                next_planes = [transpose(c + 1, j) for j in range(J)]
                 next_grouped, next_codes, next_scales = new_operands()
+                for j in range(J):
+                    regroup(transpose(c + 1, j), next_grouped, j)
             running = sums.tile([P, SUMS, J, F], F32)
             result = sums.tile([P, J, F], F32)
             for j in range(J):
-                if more:
-                    regroup(next_planes[j], next_grouped, j)
                 products = [multiply(codes, scales, j, first) for first in range(0, EXPERTS, BANK_EXPERTS)]
                 for e in reversed(range(SUMS)):
                     nc.scalar.activation(
@@ -178,8 +177,8 @@ def tile_dispatchbyvariable_pa_t_e_kernel(tc, x, W_words, W_scales, out):
                 others = [i for i in range(SUMS) if i != last]
                 nc.gpsimd.tensor_add(out=result[:, j, :], in0=running[:, others[0], j, :], in1=running[:, others[1], j, :])
                 nc.gpsimd.tensor_add(out=result[:, j, :], in0=result[:, j, :], in1=running[:, last, j, :])
-                if more:
-                    quantise(next_grouped, next_codes, next_scales, j)
             nc.sync.dma_start(out=out_chunks[c], in_=result[:])
             if more:
+                for j in range(J):
+                    quantise(next_grouped, next_codes, next_scales, j)
                 grouped, codes, scales = next_grouped, next_codes, next_scales

@@ -25,6 +25,7 @@ WORDS_PASS = K_PASS // 2
 BANK_EXPERTS = 512 // F
 J = 4
 CHUNKS = TOKENS // (P * J)
+PSUM_BANKS = 8
 SUMS = 3
 
 FLOPS = 2 * TOKENS * D * F * EXPERTS
@@ -43,8 +44,7 @@ def tile_dispatchbyvariable_pa_t_e_kernel(tc, x, W_words, W_scales, out):
         keep = ctx.enter_context(tc.tile_pool(name="keep", bufs=1))
         work = ctx.enter_context(tc.tile_pool(name="work", bufs=2))
         sums = ctx.enter_context(tc.tile_pool(name="sums", bufs=3))
-        psum_t = ctx.enter_context(tc.psum_pool(name="psum_t", bufs=J))
-        psum_mm = ctx.enter_context(tc.psum_pool(name="psum_mm", bufs=2))
+        psum = ctx.enter_context(tc.psum_pool(name="psum", bufs=PSUM_BANKS))
 
         x_sb = keep.tile([P, CHUNKS, J, D], BF16)
         w_words = keep.tile([P, PASSES, EXPERTS, F], U32, align_bytes=64)
@@ -95,7 +95,7 @@ def tile_dispatchbyvariable_pa_t_e_kernel(tc, x, W_words, W_scales, out):
 
         def transpose(c, j):
             words = x_sb[:, c, j, :].bitcast(F32)
-            planes = psum_t.tile([P, PASSES * 2, P], F32)
+            planes = psum.tile([P, PASSES * 2, P], F32, tag="bank")
             for g in range(PASSES):
                 for u in range(2):
                     nc.tensor.transpose(
@@ -119,7 +119,7 @@ def tile_dispatchbyvariable_pa_t_e_kernel(tc, x, W_words, W_scales, out):
             )
 
         def multiply(codes, scales, j, first):
-            products = psum_mm.tile([P, BANK_EXPERTS, F], F32, tag="products%d" % first)
+            products = psum.tile([P, BANK_EXPERTS, F], F32, tag="bank")
             experts = slice(first, first + BANK_EXPERTS)
             for g in range(PASSES):
                 nc.tensor.matmul_mx(
@@ -150,12 +150,13 @@ def tile_dispatchbyvariable_pa_t_e_kernel(tc, x, W_words, W_scales, out):
             more = c + 1 < CHUNKS
             if more:
                 factors(c + 1)
+                next_planes = [transpose(c + 1, j) for j in range(J)]
                 next_grouped, next_codes, next_scales = new_operands()
-                for j in range(J):
-                    regroup(transpose(c + 1, j), next_grouped, j)
             running = sums.tile([P, SUMS, J, F], F32)
             result = sums.tile([P, J, F], F32)
             for j in range(J):
+                if more:
+                    regroup(next_planes[j], next_grouped, j)
                 products = [multiply(codes, scales, j, first) for first in range(0, EXPERTS, BANK_EXPERTS)]
                 for e in reversed(range(SUMS)):
                     nc.scalar.activation(
@@ -177,8 +178,8 @@ def tile_dispatchbyvariable_pa_t_e_kernel(tc, x, W_words, W_scales, out):
                 others = [i for i in range(SUMS) if i != last]
                 nc.gpsimd.tensor_add(out=result[:, j, :], in0=running[:, others[0], j, :], in1=running[:, others[1], j, :])
                 nc.gpsimd.tensor_add(out=result[:, j, :], in0=result[:, j, :], in1=running[:, last, j, :])
+                if more:
+                    quantise(next_grouped, next_codes, next_scales, j)
             nc.sync.dma_start(out=out_chunks[c], in_=result[:])
             if more:
-                for j in range(J):
-                    quantise(next_grouped, next_codes, next_scales, j)
                 grouped, codes, scales = next_grouped, next_codes, next_scales

@@ -152,11 +152,13 @@ def tile_dispatchbyvariable_pa_t_e_kernel(tc, x, W_words, W_scales, out):
                 factors(c + 1)
                 next_planes = [transpose(c + 1, j) for j in range(J)]
                 next_grouped, next_codes, next_scales = new_operands()
+                for j in range(J):
+                    regroup(next_planes[j], next_grouped, j)
+                for j in range(J):
+                    quantise(next_grouped, next_codes, next_scales, j)
             running = sums.tile([P, SUMS, J, F], F32)
             result = sums.tile([P, J, F], F32)
             for j in range(J):
-                if more:
-                    regroup(next_planes[j], next_grouped, j)
                 products = [multiply(codes, scales, j, first) for first in range(0, EXPERTS, BANK_EXPERTS)]
                 for e in reversed(range(SUMS)):
                     nc.scalar.activation(
@@ -178,8 +180,6 @@ def tile_dispatchbyvariable_pa_t_e_kernel(tc, x, W_words, W_scales, out):
                 others = [i for i in range(SUMS) if i != last]
                 nc.gpsimd.tensor_add(out=result[:, j, :], in0=running[:, others[0], j, :], in1=running[:, others[1], j, :])
                 nc.gpsimd.tensor_add(out=result[:, j, :], in0=result[:, j, :], in1=running[:, last, j, :])
-                if more:
-                    quantise(next_grouped, next_codes, next_scales, j)
             nc.sync.dma_start(out=out_chunks[c], in_=result[:])
             if more:
                 grouped, codes, scales = next_grouped, next_codes, next_scales

@@ -56,13 +56,15 @@ def tile_dispatchbyvariable_pa_t_e_kernel(tc, x, W_words, W_scales, out):
         factor = keep.tile([P, CHUNKS * J, EXPERTS], F32)
 
         nc.vector.memset(scales_as_given[:].bitcast(I32), 0)
-        nc.sync.dma_start(out=x_sb[:, 0], in_=x_chunks[0])
+        for j in range(J):
+            nc.sync.dma_start(out=x_sb[:, 0, j], in_=x_chunks[0][:, j])
         for r in range(4):
             nc.sync.dma_start(
                 out=scales_as_given[r:P:32].rearrange("h e g n -> h (e g) n").bitcast(I32),
                 in_=scales_in[r],
             )
-        nc.sync.dma_start(out=x_sb[:, 1], in_=x_chunks[1])
+        for j in range(J):
+            nc.sync.dma_start(out=x_sb[:, 1, j], in_=x_chunks[1][:, j])
         for g in range(PASSES):
             nc.sync.dma_start(out=w_words[:, g].bitcast(I32), in_=words_in[g])
         for c in range(2, CHUNKS):
@@ -178,8 +180,12 @@ def tile_dispatchbyvariable_pa_t_e_kernel(tc, x, W_words, W_scales, out):
                     )
                 last = (EXPERTS - 1) % SUMS
                 others = [i for i in range(SUMS) if i != last]
-                nc.gpsimd.tensor_add(out=result[:, j, :], in0=running[:, others[0], j, :], in1=running[:, others[1], j, :])
-                nc.gpsimd.tensor_add(out=result[:, j, :], in0=result[:, j, :], in1=running[:, last, j, :])
-            nc.sync.dma_start(out=out_chunks[c], in_=result[:])
+                joiner = nc.gpsimd if more or j + 1 < J else nc.vector
+                joiner.tensor_add(out=result[:, j, :], in0=running[:, others[0], j, :], in1=running[:, others[1], j, :])
+                joiner.tensor_add(out=result[:, j, :], in0=result[:, j, :], in1=running[:, last, j, :])
+                if not more:
+                    nc.sync.dma_start(out=out_chunks[c][:, j, :], in_=result[:, j, :])
+            if more:
+                nc.sync.dma_start(out=out_chunks[c], in_=result[:])
             if more:
                 grouped, codes, scales = next_grouped, next_codes, next_scales

@@ -26,6 +26,7 @@ BANK_EXPERTS = 512 // F
 J = 4
 CHUNKS = TOKENS // (P * J)
 PSUM_BANKS = 8
+SORTED_TILES = 3
 SUMS = 3
 
 FLOPS = 2 * TOKENS * D * F * EXPERTS
@@ -44,6 +45,7 @@ def tile_dispatchbyvariable_pa_t_e_kernel(tc, x, W_words, W_scales, out):
         keep = ctx.enter_context(tc.tile_pool(name="keep", bufs=1))
         work = ctx.enter_context(tc.tile_pool(name="work", bufs=2))
         sums = ctx.enter_context(tc.tile_pool(name="sums", bufs=3))
+        ahead = ctx.enter_context(tc.tile_pool(name="ahead", bufs=2))
         psum = ctx.enter_context(tc.psum_pool(name="psum", bufs=PSUM_BANKS))
 
         x_sb = keep.tile([P, CHUNKS, J, D], BF16)
@@ -95,16 +97,24 @@ def tile_dispatchbyvariable_pa_t_e_kernel(tc, x, W_words, W_scales, out):
                 in1=greater[:, tiles, 1 : EXPERTS + 1],
             )
 
+        sorted_words = {}
+
+        def sort_words(c, j):
+            nc.scalar.copy(
+                out=sorted_words[c][:, j],
+                in_=x_sb[:, c, j, :].bitcast(F32).rearrange("p (g q u) -> p g u q", g=PASSES, u=2),
+            )
+
         def transpose(c, j):
             words = x_sb[:, c, j, :].bitcast(F32)
             planes = psum.tile([P, PASSES * 2, P], F32, tag="bank")
             for g in range(PASSES):
                 for u in range(2):
-                    nc.tensor.transpose(
-                        planes[:, 2 * g + u, :],
-                        words[:, WORDS_PASS * g + u : WORDS_PASS * (g + 1) : 2],
-                        ident[:],
-                    )
+                    if c in sorted_words and j < SORTED_TILES:
+                        source = sorted_words[c][:, j, g, u, :]
+                    else:
+                        source = words[:, WORDS_PASS * g + u : WORDS_PASS * (g + 1) : 2]
+                    nc.tensor.transpose(planes[:, 2 * g + u, :], source, ident[:])
             return planes
 
         def regroup(planes, grouped, j):
@@ -158,6 +168,9 @@ def tile_dispatchbyvariable_pa_t_e_kernel(tc, x, W_words, W_scales, out):
                     regroup(next_planes[j], next_grouped, j)
                 for j in range(J):
                     quantise(next_grouped, next_codes, next_scales, j)
+            if c + 2 < CHUNKS:
+                words_ahead = ahead.tile([P, SORTED_TILES, PASSES, 2, P], F32)
+                sorted_words[c + 2] = words_ahead
             running = sums.tile([P, SUMS, J, F], F32)
             result = sums.tile([P, J, F], F32)
             for j in range(J):
@@ -169,6 +182,8 @@ def tile_dispatchbyvariable_pa_t_e_kernel(tc, x, W_words, W_scales, out):
                         func=COPY,
                         scale=factor[:, c * J + j, e : e + 1],
                     )
+                if c + 2 < CHUNKS and j < SORTED_TILES:
+                    sort_words(c + 2, j)
                 for e in range(SUMS, EXPERTS):
                     nc.vector.scalar_tensor_tensor(
                         out=running[:, e % SUMS, j, :],

@@ -26,7 +26,8 @@ BANK_EXPERTS = 512 // F
 J = 4
 CHUNKS = TOKENS // (P * J)
 PSUM_BANKS = 8
-SORTED_TILES = 3
+LEAD = 1
+SORT_AFTER = {3: (2, 2), 0: (1, 0), 1: (1, 1)}
 SUMS = 3
 
 FLOPS = 2 * TOKENS * D * F * EXPERTS
@@ -58,17 +59,20 @@ def tile_dispatchbyvariable_pa_t_e_kernel(tc, x, W_words, W_scales, out):
         factor = keep.tile([P, CHUNKS * J, EXPERTS], F32)
 
         nc.vector.memset(scales_as_given[:].bitcast(I32), 0)
-        for j in range(J):
-            nc.sync.dma_start(out=x_sb[:, 0, j], in_=x_chunks[0][:, j])
+        nc.sync.dma_start(out=x_sb[:, 0, 0], in_=x_chunks[0][:, 0])
+        nc.sync.dma_start(out=x_sb[:, 0, 1], in_=x_chunks[0][:, 1])
+        nc.sync.dma_start(out=x_sb[:, 0, 2:J], in_=x_chunks[0][:, 2:J])
         for r in range(4):
             nc.sync.dma_start(
                 out=scales_as_given[r:P:32].rearrange("h e g n -> h (e g) n").bitcast(I32),
                 in_=scales_in[r],
             )
+        for first in range(0, EXPERTS, BANK_EXPERTS):
+            for g in range(PASSES):
+                experts = slice(first, first + BANK_EXPERTS)
+                nc.sync.dma_start(out=w_words[:, g, experts].bitcast(I32), in_=words_in[g][:, experts])
         for j in range(J):
             nc.sync.dma_start(out=x_sb[:, 1, j], in_=x_chunks[1][:, j])
-        for g in range(PASSES):
-            nc.sync.dma_start(out=w_words[:, g].bitcast(I32), in_=words_in[g])
         for c in range(2, CHUNKS):
             nc.sync.dma_start(out=x_sb[:, c], in_=x_chunks[c])
 
@@ -77,11 +81,6 @@ def tile_dispatchbyvariable_pa_t_e_kernel(tc, x, W_words, W_scales, out):
             nc.vector.memset(bins[:, b : b + 1], bound)
         nc.vector.memset(greater[:, :, 0:1], 1.0)
         nc.vector.memset(greater[:, :, EXPERTS : EXPERTS + 1], 0.0)
-        nc.vector.tensor_copy(
-            out=w_scales[:].bitcast(I32),
-            in_=scales_as_given[:].bitcast(I32).rearrange("p e g n -> p g e n"),
-        )
-
         def factors(c):
             tiles = slice(c * J, (c + 1) * J)
             shape = [P, J, len(BINS)]
@@ -98,8 +97,13 @@ def tile_dispatchbyvariable_pa_t_e_kernel(tc, x, W_words, W_scales, out):
             )
 
         sorted_words = {}
+        sorted_tiles = set()
 
         def sort_words(c, j):
+            if c not in sorted_words:
+                words_ahead = ahead.tile([P, J, PASSES, 2, P], F32)
+                sorted_words[c] = words_ahead
+            sorted_tiles.add((c, j))
             nc.scalar.copy(
                 out=sorted_words[c][:, j],
                 in_=x_sb[:, c, j, :].bitcast(F32).rearrange("p (g q u) -> p g u q", g=PASSES, u=2),
@@ -110,7 +114,7 @@ def tile_dispatchbyvariable_pa_t_e_kernel(tc, x, W_words, W_scales, out):
             planes = psum.tile([P, PASSES * 2, P], F32, tag="bank")
             for g in range(PASSES):
                 for u in range(2):
-                    if c in sorted_words and j < SORTED_TILES:
+                    if (c, j) in sorted_tiles:
                         source = sorted_words[c][:, j, g, u, :]
                     else:
                         source = words[:, WORDS_PASS * g + u : WORDS_PASS * (g + 1) : 2]
@@ -151,29 +155,32 @@ def tile_dispatchbyvariable_pa_t_e_kernel(tc, x, W_words, W_scales, out):
             scales = work.tile([P, J, PASSES, P], U8, align_bytes=64)
             return grouped, codes, scales
 
-        factors(0)
-        grouped, codes, scales = new_operands()
-        for j in range(J):
-            regroup(transpose(0, j), grouped, j)
-        for j in range(J):
-            quantise(grouped, codes, scales, j)
+        operands = {}
+
+        def prepare(c):
+            planes = [transpose(c, j) for j in range(J)]
+            operands[c] = new_operands()
+            grouped, codes, scales = operands[c]
+            for j in range(J):
+                regroup(planes[j], grouped, j)
+            for j in range(J):
+                quantise(grouped, codes, scales, j)
+            factors(c)
+
+        nc.vector.tensor_copy(
+            out=w_scales[:].bitcast(I32),
+            in_=scales_as_given[:].bitcast(I32).rearrange("p e g n -> p g e n"),
+        )
+        prepare(0)
 
         for c in range(CHUNKS):
-            more = c + 1 < CHUNKS
-            if more:
-                factors(c + 1)
-                next_planes = [transpose(c + 1, j) for j in range(J)]
-                next_grouped, next_codes, next_scales = new_operands()
-                for j in range(J):
-                    regroup(next_planes[j], next_grouped, j)
-                for j in range(J):
-                    quantise(next_grouped, next_codes, next_scales, j)
-            if c + 2 < CHUNKS:
-                words_ahead = ahead.tile([P, SORTED_TILES, PASSES, 2, P], F32)
-                sorted_words[c + 2] = words_ahead
+            final = c + 1 == CHUNKS
+            grouped, codes, scales = operands[c]
             running = sums.tile([P, SUMS, J, F], F32)
             result = sums.tile([P, J, F], F32)
             for j in range(J):
+                if j == J - LEAD and not final:
+                    prepare(c + 1)
                 products = [multiply(codes, scales, j, first) for first in range(0, EXPERTS, BANK_EXPERTS)]
                 for e in reversed(range(SUMS)):
                     nc.scalar.activation(
@@ -182,8 +189,10 @@ def tile_dispatchbyvariable_pa_t_e_kernel(tc, x, W_words, W_scales, out):
                         func=COPY,
                         scale=factor[:, c * J + j, e : e + 1],
                     )
-                if c + 2 < CHUNKS and j < SORTED_TILES:
-                    sort_words(c + 2, j)
+                if j in SORT_AFTER:
+                    chunks_on, tile_to_sort = SORT_AFTER[j]
+                    if c + chunks_on < CHUNKS:
+                        sort_words(c + chunks_on, tile_to_sort)
                 for e in range(SUMS, EXPERTS):
                     nc.vector.scalar_tensor_tensor(
                         out=running[:, e % SUMS, j, :],
@@ -195,12 +204,10 @@ def tile_dispatchbyvariable_pa_t_e_kernel(tc, x, W_words, W_scales, out):
                     )
                 last = (EXPERTS - 1) % SUMS
                 others = [i for i in range(SUMS) if i != last]
-                joiner = nc.gpsimd if more or j + 1 < J else nc.vector
+                joiner = nc.vector if final and j + 1 == J else nc.gpsimd
                 joiner.tensor_add(out=result[:, j, :], in0=running[:, others[0], j, :], in1=running[:, others[1], j, :])
                 joiner.tensor_add(out=result[:, j, :], in0=result[:, j, :], in1=running[:, last, j, :])
-                if not more:
+                if final:
                     nc.sync.dma_start(out=out_chunks[c][:, j, :], in_=result[:, j, :])
-            if more:
+            if not final:
                 nc.sync.dma_start(out=out_chunks[c], in_=result[:])
-            if more:
-                grouped, codes, scales = next_grouped, next_codes, next_scales

@@ -26,8 +26,11 @@ BANK_EXPERTS = 512 // F
 J = 4
 CHUNKS = TOKENS // (P * J)
 PSUM_BANKS = 8
+WARM_UP = 4
 LEAD = 1
 SORT_AFTER = {3: (2, 2), 0: (1, 0), 1: (1, 1)}
+VECTOR_SORTS_AFTER = 1
+SINGLE_JOIN_CHUNKS = 2
 SUMS = 3
 
 FLOPS = 2 * TOKENS * D * F * EXPERTS
@@ -76,6 +79,12 @@ def tile_dispatchbyvariable_pa_t_e_kernel(tc, x, W_words, W_scales, out):
         for c in range(2, CHUNKS):
             nc.sync.dma_start(out=x_sb[:, c], in_=x_chunks[c])
 
+        zeros = keep.tile([P, 512], BF16)
+        nc.gpsimd.memset(zeros[:], 0.0)
+        idle_product = psum.tile([P, 512], F32, tag="bank")
+        for i in range(WARM_UP):
+            nc.tensor.matmul(out=idle_product[:], lhsT=zeros[:, 0:P], rhs=zeros[:], start=True, stop=True)
+
         make_identity(nc, ident[:])
         for b, bound in enumerate(BINS):
             nc.vector.memset(bins[:, b : b + 1], bound)
@@ -99,12 +108,12 @@ def tile_dispatchbyvariable_pa_t_e_kernel(tc, x, W_words, W_scales, out):
         sorted_words = {}
         sorted_tiles = set()
 
-        def sort_words(c, j):
+        def sort_words(c, j, copy):
             if c not in sorted_words:
                 words_ahead = ahead.tile([P, J, PASSES, 2, P], F32)
                 sorted_words[c] = words_ahead
             sorted_tiles.add((c, j))
-            nc.scalar.copy(
+            copy(
                 out=sorted_words[c][:, j],
                 in_=x_sb[:, c, j, :].bitcast(F32).rearrange("p (g q u) -> p g u q", g=PASSES, u=2),
             )
@@ -192,7 +201,7 @@ def tile_dispatchbyvariable_pa_t_e_kernel(tc, x, W_words, W_scales, out):
                 if j in SORT_AFTER:
                     chunks_on, tile_to_sort = SORT_AFTER[j]
                     if c + chunks_on < CHUNKS:
-                        sort_words(c + chunks_on, tile_to_sort)
+                        sort_words(c + chunks_on, tile_to_sort, nc.scalar.copy)
                 for e in range(SUMS, EXPERTS):
                     nc.vector.scalar_tensor_tensor(
                         out=running[:, e % SUMS, j, :],
@@ -202,11 +211,18 @@ def tile_dispatchbyvariable_pa_t_e_kernel(tc, x, W_words, W_scales, out):
                         op0=ALU.mult,
                         op1=ALU.add,
                     )
+                if j == VECTOR_SORTS_AFTER and not final:
+                    sort_words(c + 1, J - 1, nc.vector.tensor_copy)
                 last = (EXPERTS - 1) % SUMS
                 others = [i for i in range(SUMS) if i != last]
-                joiner = nc.vector if final and j + 1 == J else nc.gpsimd
-                joiner.tensor_add(out=result[:, j, :], in0=running[:, others[0], j, :], in1=running[:, others[1], j, :])
-                joiner.tensor_add(out=result[:, j, :], in0=result[:, j, :], in1=running[:, last, j, :])
+                if c + SINGLE_JOIN_CHUNKS >= CHUNKS:
+                    tiles = slice(j, j + 1)
+                else:
+                    tiles = slice(j - 1, j + 1)
+                if c + SINGLE_JOIN_CHUNKS >= CHUNKS or j % 2 == 1:
+                    joiner = nc.vector if final and j + 1 == J else nc.gpsimd
+                    joiner.tensor_add(out=result[:, tiles], in0=running[:, others[0], tiles], in1=running[:, others[1], tiles])
+                    joiner.tensor_add(out=result[:, tiles], in0=result[:, tiles], in1=running[:, last, tiles])
                 if final:
                     nc.sync.dma_start(out=out_chunks[c][:, j, :], in_=result[:, j, :])
             if not final:

@@ -27,9 +27,8 @@ J = 4
 CHUNKS = TOKENS // (P * J)
 PSUM_BANKS = 8
 WARM_UP = 4
-LEAD = 1
-SORT_AFTER = {3: (2, 2), 0: (1, 0), 1: (1, 1)}
-VECTOR_SORTS_AFTER = 1
+RUNS = ((1,), (2, 3), (4, 5), (6, 7))
+VECTOR_JOINS = 2
 SINGLE_JOIN_CHUNKS = 2
 SUMS = 3
 
@@ -47,7 +46,7 @@ def tile_dispatchbyvariable_pa_t_e_kernel(tc, x, W_words, W_scales, out):
     with ExitStack() as ctx:
         ctx.enter_context(tc.manual_schedule())
         keep = ctx.enter_context(tc.tile_pool(name="keep", bufs=1))
-        work = ctx.enter_context(tc.tile_pool(name="work", bufs=2))
+        work = ctx.enter_context(tc.tile_pool(name="work", bufs=3))
         sums = ctx.enter_context(tc.tile_pool(name="sums", bufs=3))
         ahead = ctx.enter_context(tc.tile_pool(name="ahead", bufs=2))
         psum = ctx.enter_context(tc.psum_pool(name="psum", bufs=PSUM_BANKS))
@@ -166,21 +165,43 @@ def tile_dispatchbyvariable_pa_t_e_kernel(tc, x, W_words, W_scales, out):
 
         operands = {}
 
-        def prepare(c):
-            planes = [transpose(c, j) for j in range(J)]
-            operands[c] = new_operands()
-            grouped, codes, scales = operands[c]
-            for j in range(J):
-                regroup(planes[j], grouped, j)
-            for j in range(J):
-                quantise(grouped, codes, scales, j)
-            factors(c)
+        def prepare(chunks):
+            planes = {}
+            for c in chunks:
+                for j in range(J):
+                    planes[(c, j)] = transpose(c, j)
+            for c in chunks:
+                operands[c] = new_operands()
+                for j in range(J):
+                    regroup(planes[(c, j)], operands[c][0], j)
+            for c in chunks:
+                grouped, codes, scales = operands[c]
+                for j in range(J):
+                    quantise(grouped, codes, scales, j)
+                factors(c)
+
+        run_before = {}
+        scalar_sorts_after = {}
+        vector_sorts_after = {}
+        for chunks in RUNS:
+            a = chunks[0]
+            run_before[(a - 1, J - 1)] = chunks
+            if len(chunks) == 2:
+                b = chunks[1]
+                places = [(a - 2, J - 1), (a - 1, 0), (a - 1, 1), (a - 1, 2)]
+                for place, by_scalar, by_vector in zip(places, [(a, 0), (a, 1), (b, 0), (b, 1)], [(a, 2), (a, 3), (b, 2), (b, 3)]):
+                    scalar_sorts_after[place] = by_scalar
+                    vector_sorts_after[place] = by_vector
+            else:
+                scalar_sorts_after[(a - 1, 0)] = (a, 0)
+                scalar_sorts_after[(a - 1, 1)] = (a, 1)
+                vector_sorts_after[(a - 1, 1)] = (a, 3)
 
         nc.vector.tensor_copy(
             out=w_scales[:].bitcast(I32),
             in_=scales_as_given[:].bitcast(I32).rearrange("p e g n -> p g e n"),
         )
-        prepare(0)
+        prepare((0,))
 
         for c in range(CHUNKS):
             final = c + 1 == CHUNKS
@@ -188,8 +209,8 @@ def tile_dispatchbyvariable_pa_t_e_kernel(tc, x, W_words, W_scales, out):
             running = sums.tile([P, SUMS, J, F], F32)
             result = sums.tile([P, J, F], F32)
             for j in range(J):
-                if j == J - LEAD and not final:
-                    prepare(c + 1)
+                if (c, j) in run_before:
+                    prepare(run_before[(c, j)])
                 products = [multiply(codes, scales, j, first) for first in range(0, EXPERTS, BANK_EXPERTS)]
                 for e in reversed(range(SUMS)):
                     nc.scalar.activation(
@@ -198,10 +219,9 @@ def tile_dispatchbyvariable_pa_t_e_kernel(tc, x, W_words, W_scales, out):
                         func=COPY,
                         scale=factor[:, c * J + j, e : e + 1],
                     )
-                if j in SORT_AFTER:
-                    chunks_on, tile_to_sort = SORT_AFTER[j]
-                    if c + chunks_on < CHUNKS:
-                        sort_words(c + chunks_on, tile_to_sort, nc.scalar.copy)
+                if (c, j) in scalar_sorts_after:
+                    sort_chunk, sort_tile = scalar_sorts_after[(c, j)]
+                    sort_words(sort_chunk, sort_tile, nc.scalar.copy)
                 for e in range(SUMS, EXPERTS):
                     nc.vector.scalar_tensor_tensor(
                         out=running[:, e % SUMS, j, :],
@@ -211,8 +231,9 @@ def tile_dispatchbyvariable_pa_t_e_kernel(tc, x, W_words, W_scales, out):
                         op0=ALU.mult,
                         op1=ALU.add,
                     )
-                if j == VECTOR_SORTS_AFTER and not final:
-                    sort_words(c + 1, J - 1, nc.vector.tensor_copy)
+                if (c, j) in vector_sorts_after:
+                    sort_chunk, sort_tile = vector_sorts_after[(c, j)]
+                    sort_words(sort_chunk, sort_tile, nc.vector.tensor_copy)
                 last = (EXPERTS - 1) % SUMS
                 others = [i for i in range(SUMS) if i != last]
                 if c + SINGLE_JOIN_CHUNKS >= CHUNKS:
@@ -220,7 +241,7 @@ def tile_dispatchbyvariable_pa_t_e_kernel(tc, x, W_words, W_scales, out):
                 else:
                     tiles = slice(j - 1, j + 1)
                 if c + SINGLE_JOIN_CHUNKS >= CHUNKS or j % 2 == 1:
-                    joiner = nc.vector if final and j + 1 == J else nc.gpsimd
+                    joiner = nc.vector if final and j + VECTOR_JOINS >= J else nc.gpsimd
                     joiner.tensor_add(out=result[:, tiles], in0=running[:, others[0], tiles], in1=running[:, others[1], tiles])
                     joiner.tensor_add(out=result[:, tiles], in0=result[:, tiles], in1=running[:, last, tiles])
                 if final:

@@ -27,9 +27,9 @@ J = 4
 CHUNKS = TOKENS // (P * J)
 PSUM_BANKS = 8
 WARM_UP = 4
-RUNS = ((1,), (2, 3), (4, 5), (6, 7))
-VECTOR_JOINS = 2
-SINGLE_JOIN_CHUNKS = 2
+RUNS = ((2, 3), (4, 5), (6, 7))
+LAST_GROUPS = ((0, 4), (4, 2), (6, 2))
+LAST_SUMS = 2
 SUMS = 3
 
 FLOPS = 2 * TOKENS * D * F * EXPERTS
@@ -61,20 +61,22 @@ def tile_dispatchbyvariable_pa_t_e_kernel(tc, x, W_words, W_scales, out):
         factor = keep.tile([P, CHUNKS * J, EXPERTS], F32)
 
         nc.vector.memset(scales_as_given[:].bitcast(I32), 0)
-        nc.sync.dma_start(out=x_sb[:, 0, 0], in_=x_chunks[0][:, 0])
-        nc.sync.dma_start(out=x_sb[:, 0, 1], in_=x_chunks[0][:, 1])
-        nc.sync.dma_start(out=x_sb[:, 0, 2:J], in_=x_chunks[0][:, 2:J])
+        for j in range(J):
+            nc.sync.dma_start(out=x_sb[:, 0, j], in_=x_chunks[0][:, j])
         for r in range(4):
             nc.sync.dma_start(
                 out=scales_as_given[r:P:32].rearrange("h e g n -> h (e g) n").bitcast(I32),
                 in_=scales_in[r],
             )
-        for first in range(0, EXPERTS, BANK_EXPERTS):
+        def load_words(first):
+            experts = slice(first, first + BANK_EXPERTS)
             for g in range(PASSES):
-                experts = slice(first, first + BANK_EXPERTS)
                 nc.sync.dma_start(out=w_words[:, g, experts].bitcast(I32), in_=words_in[g][:, experts])
+
+        load_words(0)
         for j in range(J):
             nc.sync.dma_start(out=x_sb[:, 1, j], in_=x_chunks[1][:, j])
+        load_words(BANK_EXPERTS)
         for c in range(2, CHUNKS):
             nc.sync.dma_start(out=x_sb[:, c], in_=x_chunks[c])
 
@@ -89,15 +91,19 @@ def tile_dispatchbyvariable_pa_t_e_kernel(tc, x, W_words, W_scales, out):
             nc.vector.memset(bins[:, b : b + 1], bound)
         nc.vector.memset(greater[:, :, 0:1], 1.0)
         nc.vector.memset(greater[:, :, EXPERTS : EXPERTS + 1], 0.0)
-        def factors(c):
-            tiles = slice(c * J, (c + 1) * J)
-            shape = [P, J, len(BINS)]
+
+        def compare(first, last):
+            tiles = slice(first * J, (last + 1) * J)
+            shape = [P, (last + 1 - first) * J, len(BINS)]
             nc.vector.tensor_tensor(
                 out=greater[:, tiles, 1:EXPERTS],
-                in0=x_sb[:, c, :, 0:1].to_broadcast(shape),
+                in0=x_sb[:, first : last + 1, :, 0:1].rearrange("p c j k -> p (c j) k").to_broadcast(shape),
                 in1=bins[:].unsqueeze(1).to_broadcast(shape),
                 op=ALU.is_gt,
             )
+
+        def subtract(first, last):
+            tiles = slice(first * J, (last + 1) * J)
             nc.vector.tensor_sub(
                 out=factor[:, tiles, :],
                 in0=greater[:, tiles, 0:EXPERTS],
@@ -142,19 +148,23 @@ def tile_dispatchbyvariable_pa_t_e_kernel(tc, x, W_words, W_scales, out):
                 in_=grouped[:, j].rearrange("p g n t -> p (g n t)"),
             )
 
-        def multiply(codes, scales, j, first):
+        def pass_mx(products, c, j, first, g, count=BANK_EXPERTS):
+            grouped, codes, scales = operands[c]
+            experts = slice(first, first + count)
+            nc.tensor.matmul_mx(
+                out=products[:, 0:count, :].rearrange("p e f -> p (e f)"),
+                lhsT=codes[:, j, g, :].bitcast(FP8X4),
+                lhsT_scale=scales[:, j, g, :],
+                rhs=w_words[:, g, experts, :].rearrange("p e n -> p (e n)").bitcast(FP8X4),
+                rhs_scale=w_scales[:, g, experts, :].rearrange("p e n -> p (e n)"),
+                start=(g == 0),
+                stop=(g == PASSES - 1),
+            )
+
+        def multiply(c, j, first, count=BANK_EXPERTS):
             products = psum.tile([P, BANK_EXPERTS, F], F32, tag="bank")
-            experts = slice(first, first + BANK_EXPERTS)
             for g in range(PASSES):
-                nc.tensor.matmul_mx(
-                    out=products[:].rearrange("p e f -> p (e f)"),
-                    lhsT=codes[:, j, g, :].bitcast(FP8X4),
-                    lhsT_scale=scales[:, j, g, :],
-                    rhs=w_words[:, g, experts, :].rearrange("p e n -> p (e n)").bitcast(FP8X4),
-                    rhs_scale=w_scales[:, g, experts, :].rearrange("p e n -> p (e n)"),
-                    start=(g == 0),
-                    stop=(g == PASSES - 1),
-                )
+                pass_mx(products, c, j, first, g, count)
             return products
 
         def new_operands():
@@ -174,11 +184,13 @@ def tile_dispatchbyvariable_pa_t_e_kernel(tc, x, W_words, W_scales, out):
                 operands[c] = new_operands()
                 for j in range(J):
                     regroup(planes[(c, j)], operands[c][0], j)
-            for c in chunks:
-                grouped, codes, scales = operands[c]
-                for j in range(J):
-                    quantise(grouped, codes, scales, j)
-                factors(c)
+            tiles = [(c, j) for c in chunks for j in range(J)]
+            for i, (c, j) in enumerate(tiles):
+                if i == 1:
+                    compare(chunks[0], chunks[-1])
+                if i == 2:
+                    subtract(chunks[0], chunks[-1])
+                quantise(*operands[c], j)
 
         run_before = {}
         scalar_sorts_after = {}
@@ -186,64 +198,116 @@ def tile_dispatchbyvariable_pa_t_e_kernel(tc, x, W_words, W_scales, out):
         for chunks in RUNS:
             a = chunks[0]
             run_before[(a - 1, J - 1)] = chunks
-            if len(chunks) == 2:
-                b = chunks[1]
-                places = [(a - 2, J - 1), (a - 1, 0), (a - 1, 1), (a - 1, 2)]
-                for place, by_scalar, by_vector in zip(places, [(a, 0), (a, 1), (b, 0), (b, 1)], [(a, 2), (a, 3), (b, 2), (b, 3)]):
-                    scalar_sorts_after[place] = by_scalar
-                    vector_sorts_after[place] = by_vector
-            else:
-                scalar_sorts_after[(a - 1, 0)] = (a, 0)
-                scalar_sorts_after[(a - 1, 1)] = (a, 1)
-                vector_sorts_after[(a - 1, 1)] = (a, 3)
+            b = chunks[1]
+            places = [(a - 2, J - 1), (a - 1, 0), (a - 1, 1), (a - 1, 2)]
+            for place, by_scalar, by_vector in zip(places, [(a, 0), (a, 1), (b, 0), (b, 1)], [(a, 2), (a, 3), (b, 2), (b, 3)]):
+                scalar_sorts_after[place] = by_scalar
+                vector_sorts_after[place] = by_vector
 
-        nc.vector.tensor_copy(
-            out=w_scales[:].bitcast(I32),
-            in_=scales_as_given[:].bitcast(I32).rearrange("p e g n -> p g e n"),
-        )
-        prepare((0,))
-
-        for c in range(CHUNKS):
-            final = c + 1 == CHUNKS
-            grouped, codes, scales = operands[c]
+        def new_sums():
             running = sums.tile([P, SUMS, J, F], F32)
             result = sums.tile([P, J, F], F32)
+            return running, result
+
+        def start_sums(running, products, c, j, n_sums=SUMS):
+            for e in reversed(range(n_sums)):
+                nc.scalar.activation(
+                    out=running[:, e, j, :],
+                    in_=products[:, e, :],
+                    func=COPY,
+                    scale=factor[:, c * J + j, e : e + 1],
+                )
+
+        def add_experts(running, products, c, j, experts, first, n_sums=SUMS):
+            for e in experts:
+                nc.vector.scalar_tensor_tensor(
+                    out=running[:, e % n_sums, j, :],
+                    in0=products[:, e - first, :],
+                    scalar=factor[:, c * J + j, e : e + 1],
+                    in1=running[:, e % n_sums, j, :],
+                    op0=ALU.mult,
+                    op1=ALU.add,
+                )
+
+        def sort_ahead(c, j, places, copy):
+            if (c, j) in places:
+                sort_words(*places[(c, j)], copy)
+
+        def join(joiner, running, result, tiles):
+            last = (EXPERTS - 1) % SUMS
+            others = [i for i in range(SUMS) if i != last]
+            joiner.tensor_add(out=result[:, tiles], in0=running[:, others[0], tiles], in1=running[:, others[1], tiles])
+            joiner.tensor_add(out=result[:, tiles], in0=result[:, tiles], in1=running[:, last, tiles])
+
+        planes = [transpose(0, j) for j in range(J)]
+        operands[0] = new_operands()
+        for j in range(J):
+            regroup(planes[j], operands[0][0], j)
+        for j in range(J):
+            if j == 1:
+                compare(0, 0)
+                nc.vector.tensor_copy(
+                    out=w_scales[:].bitcast(I32),
+                    in_=scales_as_given[:].bitcast(I32).rearrange("p e g n -> p g e n"),
+                )
+            if j == 2:
+                subtract(0, 0)
+            quantise(*operands[0], j)
+
+        for j in range(J):
+            sort_words(1, j, nc.scalar.copy if j % 2 == 0 else nc.vector.tensor_copy)
+        running, result = new_sums()
+        banks = []
+        for j in range(J):
+            products = psum.tile([P, BANK_EXPERTS, F], F32, tag="bank")
+            banks.append(products)
+        for g in range(PASSES):
+            for j in range(J):
+                pass_mx(banks[j], 0, j, 0, g)
+        for j in range(J):
+            start_sums(running, banks[j], 0, j)
+            add_experts(running, banks[j], 0, j, range(SUMS, BANK_EXPERTS), 0)
+        compare(1, 1)
+        subtract(1, 1)
+        planes = [transpose(1, j) for j in range(J)]
+        operands[1] = new_operands()
+        for j in range(J):
+            regroup(planes[j], operands[1][0], j)
+        for j in range(J):
+            products = multiply(0, j, BANK_EXPERTS)
+            add_experts(running, products, 0, j, range(BANK_EXPERTS, EXPERTS), BANK_EXPERTS)
+            quantise(*operands[1], j)
+            sort_ahead(0, j, scalar_sorts_after, nc.scalar.copy)
+            sort_ahead(0, j, vector_sorts_after, nc.vector.tensor_copy)
+            if j % 2 == 1:
+                join(nc.gpsimd, running, result, slice(j - 1, j + 1))
+        nc.sync.dma_start(out=out_chunks[0], in_=result[:])
+
+        for c in range(1, CHUNKS):
+            final = c + 1 == CHUNKS
+            running, result = new_sums()
             for j in range(J):
                 if (c, j) in run_before:
                     prepare(run_before[(c, j)])
-                products = [multiply(codes, scales, j, first) for first in range(0, EXPERTS, BANK_EXPERTS)]
-                for e in reversed(range(SUMS)):
-                    nc.scalar.activation(
-                        out=running[:, e, j, :],
-                        in_=products[0][:, e, :],
-                        func=COPY,
-                        scale=factor[:, c * J + j, e : e + 1],
-                    )
-                if (c, j) in scalar_sorts_after:
-                    sort_chunk, sort_tile = scalar_sorts_after[(c, j)]
-                    sort_words(sort_chunk, sort_tile, nc.scalar.copy)
-                for e in range(SUMS, EXPERTS):
-                    nc.vector.scalar_tensor_tensor(
-                        out=running[:, e % SUMS, j, :],
-                        in0=products[e // BANK_EXPERTS][:, e % BANK_EXPERTS, :],
-                        scalar=factor[:, c * J + j, e : e + 1],
-                        in1=running[:, e % SUMS, j, :],
-                        op0=ALU.mult,
-                        op1=ALU.add,
-                    )
-                if (c, j) in vector_sorts_after:
-                    sort_chunk, sort_tile = vector_sorts_after[(c, j)]
-                    sort_words(sort_chunk, sort_tile, nc.vector.tensor_copy)
-                last = (EXPERTS - 1) % SUMS
-                others = [i for i in range(SUMS) if i != last]
-                if c + SINGLE_JOIN_CHUNKS >= CHUNKS:
-                    tiles = slice(j, j + 1)
-                else:
-                    tiles = slice(j - 1, j + 1)
-                if c + SINGLE_JOIN_CHUNKS >= CHUNKS or j % 2 == 1:
-                    joiner = nc.vector if final and j + VECTOR_JOINS >= J else nc.gpsimd
-                    joiner.tensor_add(out=result[:, tiles], in0=running[:, others[0], tiles], in1=running[:, others[1], tiles])
-                    joiner.tensor_add(out=result[:, tiles], in0=result[:, tiles], in1=running[:, last, tiles])
+                if final and j == J - 1:
+                    groups = [(first, count, multiply(c, j, first, count)) for first, count in LAST_GROUPS]
+                    start_sums(running, groups[0][2], c, j, LAST_SUMS)
+                    for first, count, products in groups:
+                        experts = range(max(first, LAST_SUMS), first + count)
+                        add_experts(running, products, c, j, experts, first, LAST_SUMS)
+                    nc.vector.tensor_add(out=result[:, j, :], in0=running[:, 0, j, :], in1=running[:, 1, j, :])
+                    nc.sync.dma_start(out=out_chunks[c][:, j, :], in_=result[:, j, :])
+                    continue
+                products = [multiply(c, j, first) for first in range(0, EXPERTS, BANK_EXPERTS)]
+                start_sums(running, products[0], c, j)
+                sort_ahead(c, j, scalar_sorts_after, nc.scalar.copy)
+                add_experts(running, products[0], c, j, range(SUMS, BANK_EXPERTS), 0)
+                add_experts(running, products[1], c, j, range(BANK_EXPERTS, EXPERTS), BANK_EXPERTS)
+                sort_ahead(c, j, vector_sorts_after, nc.vector.tensor_copy)
+                if final:
+                    join(nc.gpsimd, running, result, slice(j, j + 1))
+                elif j % 2 == 1:
+                    join(nc.gpsimd, running, result, slice(j - 1, j + 1))
                 if final:
                     nc.sync.dma_start(out=out_chunks[c][:, j, :], in_=result[:, j, :])
             if not final:

@@ -52,8 +52,8 @@ def tile_dispatchbyvariable_pa_t_e_kernel(tc, x, W_words, W_scales, out):
         psum = ctx.enter_context(tc.psum_pool(name="psum", bufs=PSUM_BANKS))
 
         x_sb = keep.tile([P, CHUNKS, J, D], BF16)
-        w_words = keep.tile([P, PASSES, EXPERTS, F], U32, align_bytes=64)
-        w_scales = keep.tile([P, PASSES, EXPERTS, F], U8, align_bytes=64)
+        w_words = keep.tile([P, PASSES, EXPERTS, F], U32, align_bytes=256)
+        w_scales = keep.tile([P, PASSES, EXPERTS, F], U8, align_bytes=256)
         scales_as_given = keep.tile([P, EXPERTS, PASSES, F], U8, align_bytes=64)
         ident = keep.tile([P, P], F32)
         bins = keep.tile([P, len(BINS)], F32)
@@ -169,8 +169,8 @@ def tile_dispatchbyvariable_pa_t_e_kernel(tc, x, W_words, W_scales, out):
 
         def new_operands():
             grouped = work.tile([P, J, PASSES, P, PACK], BF16, align_bytes=64)
-            codes = work.tile([P, J, PASSES, P], U32, align_bytes=64)
-            scales = work.tile([P, J, PASSES, P], U8, align_bytes=64)
+            codes = work.tile([P, J, PASSES, P], U32, align_bytes=256)
+            scales = work.tile([P, J, PASSES, P], U8, align_bytes=256)
             return grouped, codes, scales
 
         operands = {}

@@ -28,6 +28,7 @@ CHUNKS = TOKENS // (P * J)
 PSUM_BANKS = 8
 WARM_UP = 4
 RUNS = ((2, 3), (4, 5), (6, 7))
+RUN_AT = (7, 14, 21)
 LAST_GROUPS = ((0, 4), (4, 2), (6, 2))
 LAST_SUMS = 2
 SUMS = 3
@@ -175,6 +176,12 @@ def tile_dispatchbyvariable_pa_t_e_kernel(tc, x, W_words, W_scales, out):
 
         operands = {}
 
+        def scalar_tiles(chunks):
+            return [(c, j) for c in chunks for j in range(2)]
+
+        def vector_tiles(chunks):
+            return [(c, j) for c in chunks for j in range(2, J)]
+
         def prepare(chunks):
             planes = {}
             for c in chunks:
@@ -191,18 +198,19 @@ def tile_dispatchbyvariable_pa_t_e_kernel(tc, x, W_words, W_scales, out):
                 if i == 2:
                     subtract(chunks[0], chunks[-1])
                 quantise(*operands[c], j)
+                if chunks == RUNS[-2] and i % 2 == 1:
+                    sort_words(*vector_tiles(RUNS[-1])[i // 2], nc.vector.tensor_copy)
 
         run_before = {}
         scalar_sorts_after = {}
         vector_sorts_after = {}
-        for chunks in RUNS:
-            a = chunks[0]
-            run_before[(a - 1, J - 1)] = chunks
-            b = chunks[1]
-            places = [(a - 2, J - 1), (a - 1, 0), (a - 1, 1), (a - 1, 2)]
-            for place, by_scalar, by_vector in zip(places, [(a, 0), (a, 1), (b, 0), (b, 1)], [(a, 2), (a, 3), (b, 2), (b, 3)]):
-                scalar_sorts_after[place] = by_scalar
-                vector_sorts_after[place] = by_vector
+        for chunks, at in zip(RUNS, RUN_AT):
+            run_before[divmod(at, J)] = chunks
+            places = [divmod(i, J) for i in range(at - 4, at)]
+            for i, place in enumerate(places):
+                scalar_sorts_after[place] = scalar_tiles(chunks)[i]
+                if chunks != RUNS[-1]:
+                    vector_sorts_after[place] = vector_tiles(chunks)[i]
 
         def new_sums():
             running = sums.tile([P, SUMS, J, F], F32)
@@ -255,7 +263,7 @@ def tile_dispatchbyvariable_pa_t_e_kernel(tc, x, W_words, W_scales, out):
             quantise(*operands[0], j)
 
         for j in range(J):
-            sort_words(1, j, nc.scalar.copy if j % 2 == 0 else nc.vector.tensor_copy)
+            sort_words(1, j, nc.vector.tensor_copy)
         running, result = new_sums()
         banks = []
         for j in range(J):

@@ -52,14 +52,14 @@ def tile_dispatchbyvariable_pa_t_e_kernel(tc, x, W_words, W_scales, out):
         ahead = ctx.enter_context(tc.tile_pool(name="ahead", bufs=2))
         psum = ctx.enter_context(tc.psum_pool(name="psum", bufs=PSUM_BANKS))
 
-        x_sb = keep.tile([P, CHUNKS, J, D], BF16)
+        x_sb = keep.tile([P, CHUNKS, J, D], BF16, align_bytes=256)
         w_words = keep.tile([P, PASSES, EXPERTS, F], U32, align_bytes=256)
         w_scales = keep.tile([P, PASSES, EXPERTS, F], U8, align_bytes=256)
-        scales_as_given = keep.tile([P, EXPERTS, PASSES, F], U8, align_bytes=64)
-        ident = keep.tile([P, P], F32)
-        bins = keep.tile([P, len(BINS)], F32)
-        greater = keep.tile([P, CHUNKS * J, EXPERTS + 1], F32)
-        factor = keep.tile([P, CHUNKS * J, EXPERTS], F32)
+        scales_as_given = keep.tile([P, EXPERTS, PASSES, F], U8, align_bytes=256)
+        ident = keep.tile([P, P], F32, align_bytes=256)
+        bins = keep.tile([P, len(BINS)], F32, align_bytes=256)
+        greater = keep.tile([P, CHUNKS * J, EXPERTS + 1], F32, align_bytes=256)
+        factor = keep.tile([P, CHUNKS * J, EXPERTS], F32, align_bytes=256)
 
         nc.vector.memset(scales_as_given[:].bitcast(I32), 0)
         for j in range(J):
@@ -81,11 +81,15 @@ def tile_dispatchbyvariable_pa_t_e_kernel(tc, x, W_words, W_scales, out):
         for c in range(2, CHUNKS):
             nc.sync.dma_start(out=x_sb[:, c], in_=x_chunks[c])
 
-        zeros = keep.tile([P, 512], BF16)
+        zeros = keep.tile([P, 512], BF16, align_bytes=256)
         nc.gpsimd.memset(zeros[:], 0.0)
         idle_product = psum.tile([P, 512], F32, tag="bank")
-        for i in range(WARM_UP):
-            nc.tensor.matmul(out=idle_product[:], lhsT=zeros[:, 0:P], rhs=zeros[:], start=True, stop=True)
+
+        def keep_busy(count):
+            for i in range(count):
+                nc.tensor.matmul(out=idle_product[:], lhsT=zeros[:, 0:P], rhs=zeros[:], start=True, stop=True)
+
+        keep_busy(WARM_UP)
 
         make_identity(nc, ident[:])
         for b, bound in enumerate(BINS):
@@ -116,7 +120,7 @@ def tile_dispatchbyvariable_pa_t_e_kernel(tc, x, W_words, W_scales, out):
 
         def sort_words(c, j, copy):
             if c not in sorted_words:
-                words_ahead = ahead.tile([P, J, PASSES, 2, P], F32)
+                words_ahead = ahead.tile([P, J, PASSES, 2, P], F32, align_bytes=256)
                 sorted_words[c] = words_ahead
             sorted_tiles.add((c, j))
             copy(
@@ -169,7 +173,7 @@ def tile_dispatchbyvariable_pa_t_e_kernel(tc, x, W_words, W_scales, out):
             return products
 
         def new_operands():
-            grouped = work.tile([P, J, PASSES, P, PACK], BF16, align_bytes=64)
+            grouped = work.tile([P, J, PASSES, P, PACK], BF16, align_bytes=256)
             codes = work.tile([P, J, PASSES, P], U32, align_bytes=256)
             scales = work.tile([P, J, PASSES, P], U8, align_bytes=256)
             return grouped, codes, scales
@@ -213,8 +217,8 @@ def tile_dispatchbyvariable_pa_t_e_kernel(tc, x, W_words, W_scales, out):
                     vector_sorts_after[place] = vector_tiles(chunks)[i]
 
         def new_sums():
-            running = sums.tile([P, SUMS, J, F], F32)
-            result = sums.tile([P, J, F], F32)
+            running = sums.tile([P, SUMS, J, F], F32, align_bytes=256)
+            result = sums.tile([P, J, F], F32, align_bytes=256)
             return running, result
 
         def start_sums(running, products, c, j, n_sums=SUMS):
@@ -248,6 +252,7 @@ def tile_dispatchbyvariable_pa_t_e_kernel(tc, x, W_words, W_scales, out):
             joiner.tensor_add(out=result[:, tiles], in0=result[:, tiles], in1=running[:, last, tiles])
 
         planes = [transpose(0, j) for j in range(J)]
+        keep_busy(2)
         operands[0] = new_operands()
         for j in range(J):
             regroup(planes[j], operands[0][0], j)

@@ -26,11 +26,10 @@ BANK_EXPERTS = 512 // F
 J = 4
 CHUNKS = TOKENS // (P * J)
 PSUM_BANKS = 8
+KEEP_BUSY_AFTER = (1, 2)
 WARM_UP = 4
 RUNS = ((2, 3), (4, 5), (6, 7))
 RUN_AT = (7, 14, 21)
-LAST_GROUPS = ((0, 4), (4, 2), (6, 2))
-LAST_SUMS = 2
 SUMS = 3
 
 FLOPS = 2 * TOKENS * D * F * EXPERTS
@@ -221,25 +220,26 @@ def tile_dispatchbyvariable_pa_t_e_kernel(tc, x, W_words, W_scales, out):
             result = sums.tile([P, J, F], F32, align_bytes=256)
             return running, result
 
-        def start_sums(running, products, c, j, n_sums=SUMS):
-            for e in reversed(range(n_sums)):
-                nc.scalar.activation(
-                    out=running[:, e, j, :],
-                    in_=products[:, e, :],
-                    func=COPY,
-                    scale=factor[:, c * J + j, e : e + 1],
-                )
+        def scale_by_factor(total, product, c, j, e):
+            nc.scalar.activation(out=total, in_=product, func=COPY, scale=factor[:, c * J + j, e : e + 1])
 
-        def add_experts(running, products, c, j, experts, first, n_sums=SUMS):
+        def add_by_factor(total, product, c, j, e):
+            nc.vector.scalar_tensor_tensor(
+                out=total,
+                in0=product,
+                scalar=factor[:, c * J + j, e : e + 1],
+                in1=total,
+                op0=ALU.mult,
+                op1=ALU.add,
+            )
+
+        def start_sums(running, products, c, j):
+            for e in reversed(range(SUMS)):
+                scale_by_factor(running[:, e, j, :], products[:, e, :], c, j, e)
+
+        def add_experts(running, products, c, j, experts, first):
             for e in experts:
-                nc.vector.scalar_tensor_tensor(
-                    out=running[:, e % n_sums, j, :],
-                    in0=products[:, e - first, :],
-                    scalar=factor[:, c * J + j, e : e + 1],
-                    in1=running[:, e % n_sums, j, :],
-                    op0=ALU.mult,
-                    op1=ALU.add,
-                )
+                add_by_factor(running[:, e % SUMS, j, :], products[:, e - first, :], c, j, e)
 
         def sort_ahead(c, j, places, copy):
             if (c, j) in places:
@@ -251,8 +251,11 @@ def tile_dispatchbyvariable_pa_t_e_kernel(tc, x, W_words, W_scales, out):
             joiner.tensor_add(out=result[:, tiles], in0=running[:, others[0], tiles], in1=running[:, others[1], tiles])
             joiner.tensor_add(out=result[:, tiles], in0=result[:, tiles], in1=running[:, last, tiles])
 
-        planes = [transpose(0, j) for j in range(J)]
-        keep_busy(2)
+        planes = []
+        for j in range(J):
+            planes.append(transpose(0, j))
+            if j in KEEP_BUSY_AFTER:
+                keep_busy(1)
         operands[0] = new_operands()
         for j in range(J):
             regroup(planes[j], operands[0][0], j)
@@ -303,12 +306,19 @@ def tile_dispatchbyvariable_pa_t_e_kernel(tc, x, W_words, W_scales, out):
                 if (c, j) in run_before:
                     prepare(run_before[(c, j)])
                 if final and j == J - 1:
-                    groups = [(first, count, multiply(c, j, first, count)) for first, count in LAST_GROUPS]
-                    start_sums(running, groups[0][2], c, j, LAST_SUMS)
-                    for first, count, products in groups:
-                        experts = range(max(first, LAST_SUMS), first + count)
-                        add_experts(running, products, c, j, experts, first, LAST_SUMS)
-                    nc.vector.tensor_add(out=result[:, j, :], in0=running[:, 0, j, :], in1=running[:, 1, j, :])
+                    ends = keep.tile([P, BANK_EXPERTS, F], F32, align_bytes=64)
+                    first_bank = multiply(c, j, 0)
+                    second_bank = multiply(c, j, 4, 2)
+                    third_bank = multiply(c, j, 6, 2)
+                    for e in range(BANK_EXPERTS):
+                        scale_by_factor(ends[:, e, :], first_bank[:, e, :], c, j, e)
+                    add_by_factor(ends[:, 0, :], second_bank[:, 0, :], c, j, 4)
+                    add_by_factor(ends[:, 1, :], second_bank[:, 1, :], c, j, 5)
+                    add_by_factor(ends[:, 2, :], third_bank[:, 0, :], c, j, 6)
+                    nc.vector.tensor_add(out=ends[:, 0, :], in0=ends[:, 0, :], in1=ends[:, 1, :])
+                    add_by_factor(ends[:, 3, :], third_bank[:, 1, :], c, j, 7)
+                    nc.vector.tensor_add(out=ends[:, 0, :], in0=ends[:, 0, :], in1=ends[:, 2, :])
+                    nc.vector.tensor_add(out=result[:, j, :], in0=ends[:, 0, :], in1=ends[:, 3, :])
                     nc.sync.dma_start(out=out_chunks[c][:, j, :], in_=result[:, j, :])
                     continue
                 products = [multiply(c, j, first) for first in range(0, EXPERTS, BANK_EXPERTS)]
@@ -317,11 +327,13 @@ def tile_dispatchbyvariable_pa_t_e_kernel(tc, x, W_words, W_scales, out):
                 add_experts(running, products[0], c, j, range(SUMS, BANK_EXPERTS), 0)
                 add_experts(running, products[1], c, j, range(BANK_EXPERTS, EXPERTS), BANK_EXPERTS)
                 sort_ahead(c, j, vector_sorts_after, nc.vector.tensor_copy)
-                if final:
-                    join(nc.gpsimd, running, result, slice(j, j + 1))
-                elif j % 2 == 1:
+                if j % 2 == 1:
                     join(nc.gpsimd, running, result, slice(j - 1, j + 1))
-                if final:
+                if final and j == J - 2:
+                    join(nc.gpsimd, running, result, slice(j, j + 1))
+                if final and j == 1:
+                    nc.sync.dma_start(out=out_chunks[c][:, 0:2, :], in_=result[:, 0:2, :])
+                if final and j == J - 2:
                     nc.sync.dma_start(out=out_chunks[c][:, j, :], in_=result[:, j, :])
             if not final:
                 nc.sync.dma_start(out=out_chunks[c], in_=result[:])

@@ -63,11 +63,16 @@ def tile_dispatchbyvariable_pa_t_e_kernel(tc, x, W_words, W_scales, out):
         nc.vector.memset(scales_as_given[:].bitcast(I32), 0)
         for j in range(J):
             nc.sync.dma_start(out=x_sb[:, 0, j], in_=x_chunks[0][:, j])
-        for r in range(4):
-            nc.sync.dma_start(
-                out=scales_as_given[r:P:32].rearrange("h e g n -> h (e g) n").bitcast(I32),
-                in_=scales_in[r],
-            )
+        def load_scales(first):
+            experts = slice(first, first + BANK_EXPERTS)
+            groups = slice(first * PASSES, (first + BANK_EXPERTS) * PASSES)
+            for r in range(4):
+                nc.sync.dma_start(
+                    out=scales_as_given[r:P:32, experts].rearrange("h e g n -> h (e g) n").bitcast(I32),
+                    in_=scales_in[r][:, groups],
+                )
+
+        load_scales(0)
         def load_words(first):
             experts = slice(first, first + BANK_EXPERTS)
             for g in range(PASSES):
@@ -76,6 +81,7 @@ def tile_dispatchbyvariable_pa_t_e_kernel(tc, x, W_words, W_scales, out):
         load_words(0)
         for j in range(J):
             nc.sync.dma_start(out=x_sb[:, 1, j], in_=x_chunks[1][:, j])
+        load_scales(BANK_EXPERTS)
         load_words(BANK_EXPERTS)
         for c in range(2, CHUNKS):
             nc.sync.dma_start(out=x_sb[:, c], in_=x_chunks[c])
@@ -251,6 +257,13 @@ def tile_dispatchbyvariable_pa_t_e_kernel(tc, x, W_words, W_scales, out):
             joiner.tensor_add(out=result[:, tiles], in0=running[:, others[0], tiles], in1=running[:, others[1], tiles])
             joiner.tensor_add(out=result[:, tiles], in0=result[:, tiles], in1=running[:, last, tiles])
 
+        def sort_scales(first):
+            experts = slice(first, first + BANK_EXPERTS)
+            nc.vector.tensor_copy(
+                out=w_scales[:, :, experts].bitcast(I32),
+                in_=scales_as_given[:, experts].bitcast(I32).rearrange("p e g n -> p g e n"),
+            )
+
         planes = []
         for j in range(J):
             planes.append(transpose(0, j))
@@ -262,10 +275,7 @@ def tile_dispatchbyvariable_pa_t_e_kernel(tc, x, W_words, W_scales, out):
         for j in range(J):
             if j == 1:
                 compare(0, 0)
-                nc.vector.tensor_copy(
-                    out=w_scales[:].bitcast(I32),
-                    in_=scales_as_given[:].bitcast(I32).rearrange("p e g n -> p g e n"),
-                )
+                sort_scales(0)
             if j == 2:
                 subtract(0, 0)
             quantise(*operands[0], j)
@@ -283,6 +293,8 @@ def tile_dispatchbyvariable_pa_t_e_kernel(tc, x, W_words, W_scales, out):
         for j in range(J):
             start_sums(running, banks[j], 0, j)
             add_experts(running, banks[j], 0, j, range(SUMS, BANK_EXPERTS), 0)
+            if j == 1:
+                sort_scales(BANK_EXPERTS)
         compare(1, 1)
         subtract(1, 1)
         planes = [transpose(1, j) for j in range(J)]

@@ -26,7 +26,7 @@ BANK_EXPERTS = 512 // F
 J = 4
 CHUNKS = TOKENS // (P * J)
 PSUM_BANKS = 8
-KEEP_BUSY_AFTER = (1, 2)
+KEEP_BUSY_AFTER = (1, 2, 3)
 WARM_UP = 4
 RUNS = ((2, 3), (4, 5), (6, 7))
 RUN_AT = (7, 14, 21)

from contextlib import ExitStack

import concourse.mybir as mybir
from concourse.masks import make_identity

F32 = mybir.dt.float32
BF16 = mybir.dt.bfloat16
I32 = mybir.dt.int32
U32 = mybir.dt.uint32
U8 = mybir.dt.uint8
FP8X4 = mybir.dt.float8_e4m3fn_x4
ALU = mybir.AluOpType
COPY = mybir.ActivationFunctionType.Copy

P = 128
TOKENS = 4 * 1024
D = 1024
F = 128
EXPERTS = 8
BINS = (-1.5, -1.0, -0.5, 0.0, 0.5, 1.0, 1.5)
PACK = 4
K_PASS = P * PACK
PASSES = D // K_PASS
WORDS_PASS = K_PASS // 2
BANK_EXPERTS = 512 // F
J = 4
CHUNKS = TOKENS // (P * J)
PSUM_BANKS = 8
KEEP_BUSY_AFTER = (1, 2, 3)
WARM_UP = 4
RUNS = ((2, 3), (4, 5), (6, 7))
RUN_AT = (7, 14, 21)
SUMS = 3

FLOPS = 2 * TOKENS * D * F * EXPERTS


def tile_dispatchbyvariable_pa_t_e_kernel(tc, x, W_words, W_scales, out):
    nc = tc.nc
    x_chunks = x.rearrange("b t k -> (b t) k").rearrange("(c p j) k -> c p j k", p=P, j=J)
    out_chunks = out.rearrange("b t f -> (b t) f").rearrange("(c p j) f -> c p j f", p=P, j=J)
    words_in = W_words.rearrange("a p n t -> a p (n t)").bitcast(I32)
    words_in = words_in.rearrange("(e g) p n -> g p e n", g=PASSES)
    scales_in = W_scales.bitcast(I32).rearrange("a (h r) n -> r h a n", r=4)

    with ExitStack() as ctx:
        ctx.enter_context(tc.manual_schedule())
        keep = ctx.enter_context(tc.tile_pool(name="keep", bufs=1))
        work = ctx.enter_context(tc.tile_pool(name="work", bufs=3))
        sums = ctx.enter_context(tc.tile_pool(name="sums", bufs=3))
        ahead = ctx.enter_context(tc.tile_pool(name="ahead", bufs=2))
        psum = ctx.enter_context(tc.psum_pool(name="psum", bufs=PSUM_BANKS))

        x_sb = keep.tile([P, CHUNKS, J, D], BF16, align_bytes=256)
        w_words = keep.tile([P, PASSES, EXPERTS, F], U32, align_bytes=256)
        w_scales = keep.tile([P, PASSES, EXPERTS, F], U8, align_bytes=256)
        scales_as_given = keep.tile([P, EXPERTS, PASSES, F], U8, align_bytes=256)
        ident = keep.tile([P, P], F32, align_bytes=256)
        bins = keep.tile([P, len(BINS)], F32, align_bytes=256)
        greater = keep.tile([P, CHUNKS * J, EXPERTS + 1], F32, align_bytes=256)
        factor = keep.tile([P, CHUNKS * J, EXPERTS], F32, align_bytes=256)

        nc.vector.memset(scales_as_given[:].bitcast(I32), 0)
        for j in range(J):
            nc.sync.dma_start(out=x_sb[:, 0, j], in_=x_chunks[0][:, j])
        def load_scales(first):
            experts = slice(first, first + BANK_EXPERTS)
            groups = slice(first * PASSES, (first + BANK_EXPERTS) * PASSES)
            for r in range(4):
                nc.sync.dma_start(
                    out=scales_as_given[r:P:32, experts].rearrange("h e g n -> h (e g) n").bitcast(I32),
                    in_=scales_in[r][:, groups],
                )

        load_scales(0)
        def load_words(first):
            experts = slice(first, first + BANK_EXPERTS)
            for g in range(PASSES):
                nc.sync.dma_start(out=w_words[:, g, experts].bitcast(I32), in_=words_in[g][:, experts])

        load_words(0)
        for j in range(J):
            nc.sync.dma_start(out=x_sb[:, 1, j], in_=x_chunks[1][:, j])
        load_scales(BANK_EXPERTS)
        load_words(BANK_EXPERTS)
        for c in range(2, CHUNKS):
            nc.sync.dma_start(out=x_sb[:, c], in_=x_chunks[c])

        zeros = keep.tile([P, 512], BF16, align_bytes=256)
        nc.gpsimd.memset(zeros[:], 0.0)
        idle_product = psum.tile([P, 512], F32, tag="bank")

        def keep_busy(count):
            for i in range(count):
                nc.tensor.matmul(out=idle_product[:], lhsT=zeros[:, 0:P], rhs=zeros[:], start=True, stop=True)

        keep_busy(WARM_UP)

        make_identity(nc, ident[:])
        for b, bound in enumerate(BINS):
            nc.vector.memset(bins[:, b : b + 1], bound)
        nc.vector.memset(greater[:, :, 0:1], 1.0)
        nc.vector.memset(greater[:, :, EXPERTS : EXPERTS + 1], 0.0)

        def compare(first, last):
            tiles = slice(first * J, (last + 1) * J)
            shape = [P, (last + 1 - first) * J, len(BINS)]
            nc.vector.tensor_tensor(
                out=greater[:, tiles, 1:EXPERTS],
                in0=x_sb[:, first : last + 1, :, 0:1].rearrange("p c j k -> p (c j) k").to_broadcast(shape),
                in1=bins[:].unsqueeze(1).to_broadcast(shape),
                op=ALU.is_gt,
            )

        def subtract(first, last):
            tiles = slice(first * J, (last + 1) * J)
            nc.vector.tensor_sub(
                out=factor[:, tiles, :],
                in0=greater[:, tiles, 0:EXPERTS],
                in1=greater[:, tiles, 1 : EXPERTS + 1],
            )

        sorted_words = {}
        sorted_tiles = set()

        def sort_words(c, j, copy):
            if c not in sorted_words:
                words_ahead = ahead.tile([P, J, PASSES, 2, P], F32, align_bytes=256)
                sorted_words[c] = words_ahead
            sorted_tiles.add((c, j))
            copy(
                out=sorted_words[c][:, j],
                in_=x_sb[:, c, j, :].bitcast(F32).rearrange("p (g q u) -> p g u q", g=PASSES, u=2),
            )

        def transpose(c, j):
            words = x_sb[:, c, j, :].bitcast(F32)
            planes = psum.tile([P, PASSES * 2, P], F32, tag="bank")
            for g in range(PASSES):
                for u in range(2):
                    if (c, j) in sorted_tiles:
                        source = sorted_words[c][:, j, g, u, :]
                    else:
                        source = words[:, WORDS_PASS * g + u : WORDS_PASS * (g + 1) : 2]
                    nc.tensor.transpose(planes[:, 2 * g + u, :], source, ident[:])
            return planes

        def regroup(planes, grouped, j):
            nc.scalar.copy(
                out=grouped[:, j].bitcast(F32),
                in_=planes[:].rearrange("p (g u) n -> p g n u", u=2),
            )

        def quantise(grouped, codes, scales, j):
            nc.vector.quantize_mx(
                out=codes[:, j].rearrange("p g n -> p (g n)").bitcast(FP8X4),
                scales=scales[:, j].rearrange("p g n -> p (g n)"),
                in_=grouped[:, j].rearrange("p g n t -> p (g n t)"),
            )

        def pass_mx(products, c, j, first, g, count=BANK_EXPERTS):
            grouped, codes, scales = operands[c]
            experts = slice(first, first + count)
            nc.tensor.matmul_mx(
                out=products[:, 0:count, :].rearrange("p e f -> p (e f)"),
                lhsT=codes[:, j, g, :].bitcast(FP8X4),
                lhsT_scale=scales[:, j, g, :],
                rhs=w_words[:, g, experts, :].rearrange("p e n -> p (e n)").bitcast(FP8X4),
                rhs_scale=w_scales[:, g, experts, :].rearrange("p e n -> p (e n)"),
                start=(g == 0),
                stop=(g == PASSES - 1),
            )

        def multiply(c, j, first, count=BANK_EXPERTS):
            products = psum.tile([P, BANK_EXPERTS, F], F32, tag="bank")
            for g in range(PASSES):
                pass_mx(products, c, j, first, g, count)
            return products

        def new_operands():
            grouped = work.tile([P, J, PASSES, P, PACK], BF16, align_bytes=256)
            codes = work.tile([P, J, PASSES, P], U32, align_bytes=256)
            scales = work.tile([P, J, PASSES, P], U8, align_bytes=256)
            return grouped, codes, scales

        operands = {}

        def scalar_tiles(chunks):
            return [(c, j) for c in chunks for j in range(2)]

        def vector_tiles(chunks):
            return [(c, j) for c in chunks for j in range(2, J)]

        def prepare(chunks):
            planes = {}
            for c in chunks:
                for j in range(J):
                    planes[(c, j)] = transpose(c, j)
            for c in chunks:
                operands[c] = new_operands()
                for j in range(J):
                    regroup(planes[(c, j)], operands[c][0], j)
            tiles = [(c, j) for c in chunks for j in range(J)]
            for i, (c, j) in enumerate(tiles):
                if i == 1:
                    compare(chunks[0], chunks[-1])
                if i == 2:
                    subtract(chunks[0], chunks[-1])
                quantise(*operands[c], j)
                if chunks == RUNS[-2] and i % 2 == 1:
                    sort_words(*vector_tiles(RUNS[-1])[i // 2], nc.vector.tensor_copy)

        run_before = {}
        scalar_sorts_after = {}
        vector_sorts_after = {}
        for chunks, at in zip(RUNS, RUN_AT):
            run_before[divmod(at, J)] = chunks
            places = [divmod(i, J) for i in range(at - 4, at)]
            for i, place in enumerate(places):
                scalar_sorts_after[place] = scalar_tiles(chunks)[i]
                if chunks != RUNS[-1]:
                    vector_sorts_after[place] = vector_tiles(chunks)[i]

        def new_sums():
            running = sums.tile([P, SUMS, J, F], F32, align_bytes=256)
            result = sums.tile([P, J, F], F32, align_bytes=256)
            return running, result

        def scale_by_factor(total, product, c, j, e):
            nc.scalar.activation(out=total, in_=product, func=COPY, scale=factor[:, c * J + j, e : e + 1])

        def add_by_factor(total, product, c, j, e):
            nc.vector.scalar_tensor_tensor(
                out=total,
                in0=product,
                scalar=factor[:, c * J + j, e : e + 1],
                in1=total,
                op0=ALU.mult,
                op1=ALU.add,
            )

        def start_sums(running, products, c, j):
            for e in reversed(range(SUMS)):
                scale_by_factor(running[:, e, j, :], products[:, e, :], c, j, e)

        def add_experts(running, products, c, j, experts, first):
            for e in experts:
                add_by_factor(running[:, e % SUMS, j, :], products[:, e - first, :], c, j, e)

        def sort_ahead(c, j, places, copy):
            if (c, j) in places:
                sort_words(*places[(c, j)], copy)

        def join(joiner, running, result, tiles):
            last = (EXPERTS - 1) % SUMS
            others = [i for i in range(SUMS) if i != last]
            joiner.tensor_add(out=result[:, tiles], in0=running[:, others[0], tiles], in1=running[:, others[1], tiles])
            joiner.tensor_add(out=result[:, tiles], in0=result[:, tiles], in1=running[:, last, tiles])

        def sort_scales(first):
            experts = slice(first, first + BANK_EXPERTS)
            nc.vector.tensor_copy(
                out=w_scales[:, :, experts].bitcast(I32),
                in_=scales_as_given[:, experts].bitcast(I32).rearrange("p e g n -> p g e n"),
            )

        planes = []
        for j in range(J):
            planes.append(transpose(0, j))
            if j in KEEP_BUSY_AFTER:
                keep_busy(1)
        operands[0] = new_operands()
        for j in range(J):
            regroup(planes[j], operands[0][0], j)
        for j in range(J):
            if j == 1:
                compare(0, 0)
                sort_scales(0)
            if j == 2:
                subtract(0, 0)
            quantise(*operands[0], j)

        for j in range(J):
            sort_words(1, j, nc.vector.tensor_copy)
        running, result = new_sums()
        banks = []
        for j in range(J):
            products = psum.tile([P, BANK_EXPERTS, F], F32, tag="bank")
            banks.append(products)
        for g in range(PASSES):
            for j in range(J):
                pass_mx(banks[j], 0, j, 0, g)
        for j in range(J):
            start_sums(running, banks[j], 0, j)
            add_experts(running, banks[j], 0, j, range(SUMS, BANK_EXPERTS), 0)
            if j == 1:
                sort_scales(BANK_EXPERTS)
        compare(1, 1)
        subtract(1, 1)
        planes = [transpose(1, j) for j in range(J)]
        operands[1] = new_operands()
        for j in range(J):
            regroup(planes[j], operands[1][0], j)
        for j in range(J):
            products = multiply(0, j, BANK_EXPERTS)
            add_experts(running, products, 0, j, range(BANK_EXPERTS, EXPERTS), BANK_EXPERTS)
            quantise(*operands[1], j)
            sort_ahead(0, j, scalar_sorts_after, nc.scalar.copy)
            sort_ahead(0, j, vector_sorts_after, nc.vector.tensor_copy)
            if j % 2 == 1:
                join(nc.gpsimd, running, result, slice(j - 1, j + 1))
        nc.sync.dma_start(out=out_chunks[0], in_=result[:])

        for c in range(1, CHUNKS):
            final = c + 1 == CHUNKS
            running, result = new_sums()
            for j in range(J):
                if (c, j) in run_before:
                    prepare(run_before[(c, j)])
                if final and j == J - 1:
                    ends = keep.tile([P, BANK_EXPERTS, F], F32, align_bytes=64)
                    first_bank = multiply(c, j, 0)
                    second_bank = multiply(c, j, 4, 2)
                    third_bank = multiply(c, j, 6, 2)
                    for e in range(BANK_EXPERTS):
                        scale_by_factor(ends[:, e, :], first_bank[:, e, :], c, j, e)
                    add_by_factor(ends[:, 0, :], second_bank[:, 0, :], c, j, 4)
                    add_by_factor(ends[:, 1, :], second_bank[:, 1, :], c, j, 5)
                    add_by_factor(ends[:, 2, :], third_bank[:, 0, :], c, j, 6)
                    nc.vector.tensor_add(out=ends[:, 0, :], in0=ends[:, 0, :], in1=ends[:, 1, :])
                    add_by_factor(ends[:, 3, :], third_bank[:, 1, :], c, j, 7)
                    nc.vector.tensor_add(out=ends[:, 0, :], in0=ends[:, 0, :], in1=ends[:, 2, :])
                    nc.vector.tensor_add(out=result[:, j, :], in0=ends[:, 0, :], in1=ends[:, 3, :])
                    nc.sync.dma_start(out=out_chunks[c][:, j, :], in_=result[:, j, :])
                    continue
                products = [multiply(c, j, first) for first in range(0, EXPERTS, BANK_EXPERTS)]
                start_sums(running, products[0], c, j)
                sort_ahead(c, j, scalar_sorts_after, nc.scalar.copy)
                add_experts(running, products[0], c, j, range(SUMS, BANK_EXPERTS), 0)
                add_experts(running, products[1], c, j, range(BANK_EXPERTS, EXPERTS), BANK_EXPERTS)
                sort_ahead(c, j, vector_sorts_after, nc.vector.tensor_copy)
                if j % 2 == 1:
                    join(nc.gpsimd, running, result, slice(j - 1, j + 1))
                if final and j == J - 2:
                    join(nc.gpsimd, running, result, slice(j, j + 1))
                if final and j == 1:
                    nc.sync.dma_start(out=out_chunks[c][:, 0:2, :], in_=result[:, 0:2, :])
                if final and j == J - 2:
                    nc.sync.dma_start(out=out_chunks[c][:, j, :], in_=result[:, j, :])
            if not final:
                nc.sync.dma_start(out=out_chunks[c], in_=result[:])
